import numpy as np
import ml_dtypes

BF16 = ml_dtypes.bfloat16


def bf(x):
    return np.asarray(x, np.float32).astype(BF16)


def f32(x):
    return np.asarray(x, np.float32)


def f64(x):
    return np.asarray(x).astype(np.float64)


def striped(idx):
    return np.tile(idx.reshape(-1, 16).T, (8, 1))


C, S, P, L, N = 256, 256, 64, 8, 512
KEEP = 0.5


def setup_inputs():
    table = f32(np.random.standard_normal((C, S)))
    h = f32(np.random.standard_normal((C, N)))
    hmask = f32(np.tile(np.random.random((1, N)) < KEEP, (C, 1)))
    idx = np.random.permutation(np.tile(np.arange(S), 2))[:N]
    return {"table": table, "h": h, "hmask": hmask, "offs": striped(idx)}


def reference(table, h, hmask, offs):
    idx = offs[:16].T.reshape(-1)
    t = f64(table)[:, idx] + f64(h) * f64(hmask)
    return t.reshape(C, P, L).sum(axis=2)

@@ -1,0 +1,52 @@
+import concourse.mybir as mybir
+
+F32 = mybir.dt.float32
+U16 = mybir.dt.uint16
+ADD = mybir.AluOpType.add
+MULT = mybir.AluOpType.mult
+
+P = 128
+C = 256
+S = 256
+N = 512
+L = 8
+PATCHES = N // L
+PIECE = S
+PER_COLUMN = 16
+
+
+def tile_patchembedder_kernel(tc, table, h, hmask, offs, out):
+    nc = tc.nc
+    with tc.tile_pool(name="held", bufs=1) as held, tc.tile_pool(name="work", bufs=2) as work:
+        offsets = held.tile([P, N // PER_COLUMN], U16, name="offsets")
+        nc.sync.dma_start(offsets[:], offs)
+
+        for block in range(C // P):
+            rows = slice(block * P, (block + 1) * P)
+
+            window = work.tile([P, S], F32, name="window")
+            bigram = work.tile([P, N], F32, name="bigram")
+            mask = work.tile([P, N], F32, name="mask")
+            nc.sync.dma_start(window[:], table[rows, :])
+            nc.scalar.dma_start(bigram[:], h[rows, :])
+            nc.sync.dma_start(mask[:], hmask[rows, :])
+
+            masked = work.tile([P, N], F32, name="masked")
+            nc.vector.tensor_tensor(masked[:], bigram[:], mask[:], MULT)
+
+            entries = work.tile([P, N], F32, name="entries")
+            for start in range(0, N, PIECE):
+                piece = slice(start, start + PIECE)
+                piece_offsets = offsets[:, start // PER_COLUMN : (start + PIECE) // PER_COLUMN]
+                nc.vector.tensor_tensor(
+                    entries[:, piece], window[:].indirect(piece_offsets), masked[:, piece], ADD
+                )
+
+            sums = work.tile([P, PATCHES], F32, name="sums")
+            nc.vector.tensor_reduce(
+                sums[:],
+                entries[:].rearrange("c (p l) -> c p l", l=L),
+                mybir.AxisListType.X,
+                ADD,
+            )
+            nc.scalar.dma_start(out[rows, :], sums[:])

@@ -10,43 +10,45 @@ C = 256
 S = 256
 N = 512
 L = 8
-PATCHES = N // L
 PIECE = S
 PER_COLUMN = 16
+BLOCKS = C // P
+PIECES = N // PIECE
 
 
 def tile_patchembedder_kernel(tc, table, h, hmask, offs, out):
     nc = tc.nc
-    with tc.tile_pool(name="held", bufs=1) as held, tc.tile_pool(name="work", bufs=2) as work:
+    with tc.tile_pool(name="held", bufs=1) as held:
         offsets = held.tile([P, N // PER_COLUMN], U16, name="offsets")
-        nc.sync.dma_start(offsets[:], offs)
+        window = [held.tile([P, S], F32, name=f"window{b}") for b in range(BLOCKS)]
+        mask = [[held.tile([P, PIECE], F32, name=f"mask{b}{i}") for i in range(PIECES)] for b in range(BLOCKS)]
+        bigram = [[held.tile([P, PIECE], F32, name=f"bigram{b}{i}") for i in range(PIECES)] for b in range(BLOCKS)]
 
-        for block in range(C // P):
-            rows = slice(block * P, (block + 1) * P)
+        for b in range(BLOCKS):
+            rows = slice(b * P, (b + 1) * P)
+            for i in range(PIECES):
+                cols = slice(i * PIECE, (i + 1) * PIECE)
+                nc.sync.dma_start(mask[b][i][:], hmask[rows, cols])
+                nc.scalar.dma_start(bigram[b][i][:], h[rows, cols])
+                if i == 0:
+                    if b == 0:
+                        nc.sync.dma_start(offsets[:], offs)
+                    (nc.sync, nc.scalar)[b % 2].dma_start(window[b][:], table[rows, :])
 
-            window = work.tile([P, S], F32, name="window")
-            bigram = work.tile([P, N], F32, name="bigram")
-            mask = work.tile([P, N], F32, name="mask")
-            nc.sync.dma_start(window[:], table[rows, :])
-            nc.scalar.dma_start(bigram[:], h[rows, :])
-            nc.sync.dma_start(mask[:], hmask[rows, :])
+        for b in range(BLOCKS):
+            sums = held.tile([P, N // L], F32, name=f"sums{b}")
+            for i in range(PIECES):
+                masked = held.tile([P, PIECE], F32, name=f"masked{b}{i}")
+                nc.vector.tensor_tensor(masked[:], bigram[b][i][:], mask[b][i][:], MULT)
 
-            masked = work.tile([P, N], F32, name="masked")
-            nc.vector.tensor_tensor(masked[:], bigram[:], mask[:], MULT)
+                entries = held.tile([P, PIECE], F32, name=f"entries{b}{i}")
+                piece_offsets = offsets[:, i * PIECE // PER_COLUMN : (i + 1) * PIECE // PER_COLUMN]
+                nc.vector.tensor_tensor(entries[:], window[b][:].indirect(piece_offsets), masked[:], ADD)
 
-            entries = work.tile([P, N], F32, name="entries")
-            for start in range(0, N, PIECE):
-                piece = slice(start, start + PIECE)
-                piece_offsets = offsets[:, start // PER_COLUMN : (start + PIECE) // PER_COLUMN]
-                nc.vector.tensor_tensor(
-                    entries[:, piece], window[:].indirect(piece_offsets), masked[:, piece], ADD
+                nc.vector.tensor_reduce(
+                    sums[:, i * PIECE // L : (i + 1) * PIECE // L],
+                    entries[:].rearrange("c (p l) -> c p l", l=L),
+                    mybir.AxisListType.X,
+                    ADD,
                 )
-
-            sums = work.tile([P, PATCHES], F32, name="sums")
-            nc.vector.tensor_reduce(
-                sums[:],
-                entries[:].rearrange("c (p l) -> c p l", l=L),
-                mybir.AxisListType.X,
-                ADD,
-            )
-            nc.scalar.dma_start(out[rows, :], sums[:])
+            nc.sync.dma_start(out[b * P : (b + 1) * P, :], sums[:])

@@ -18,37 +18,50 @@ PIECES = N // PIECE
 
 def tile_patchembedder_kernel(tc, table, h, hmask, offs, out):
     nc = tc.nc
+    units = [(b, i) for b in range(BLOCKS) for i in range(PIECES)]
+
     with tc.tile_pool(name="held", bufs=1) as held:
         offsets = held.tile([P, N // PER_COLUMN], U16, name="offsets")
         window = [held.tile([P, S], F32, name=f"window{b}") for b in range(BLOCKS)]
-        mask = [[held.tile([P, PIECE], F32, name=f"mask{b}{i}") for i in range(PIECES)] for b in range(BLOCKS)]
-        bigram = [[held.tile([P, PIECE], F32, name=f"bigram{b}{i}") for i in range(PIECES)] for b in range(BLOCKS)]
+        sums = [held.tile([P, N // L], F32, name=f"sums{b}") for b in range(BLOCKS)]
+        mask = {u: held.tile([P, PIECE], F32, name=f"mask{u[0]}{u[1]}") for u in units}
+        bigram = {u: held.tile([P, PIECE], F32, name=f"bigram{u[0]}{u[1]}") for u in units}
+        masked = {u: held.tile([P, PIECE], F32, name=f"masked{u[0]}{u[1]}") for u in units}
+        entries = {u: held.tile([P, PIECE], F32, name=f"entries{u[0]}{u[1]}") for u in units}
 
-        for b in range(BLOCKS):
+        for b, i in units:
             rows = slice(b * P, (b + 1) * P)
-            for i in range(PIECES):
-                cols = slice(i * PIECE, (i + 1) * PIECE)
-                nc.sync.dma_start(mask[b][i][:], hmask[rows, cols])
-                nc.scalar.dma_start(bigram[b][i][:], h[rows, cols])
-                if i == 0:
-                    if b == 0:
-                        nc.sync.dma_start(offsets[:], offs)
-                    (nc.sync, nc.scalar)[b % 2].dma_start(window[b][:], table[rows, :])
+            cols = slice(i * PIECE, (i + 1) * PIECE)
+            nc.sync.dma_start(mask[b, i][:], hmask[rows, cols])
+            nc.scalar.dma_start(bigram[b, i][:], h[rows, cols])
+            if i == 0:
+                if b == 0:
+                    nc.sync.dma_start(offsets[:], offs)
+                (nc.sync, nc.scalar)[b % 2].dma_start(window[b][:], table[rows, :])
 
-        for b in range(BLOCKS):
-            sums = held.tile([P, N // L], F32, name=f"sums{b}")
-            for i in range(PIECES):
-                masked = held.tile([P, PIECE], F32, name=f"masked{b}{i}")
-                nc.vector.tensor_tensor(masked[:], bigram[b][i][:], mask[b][i][:], MULT)
+        def product(u):
+            nc.vector.tensor_tensor(masked[u][:], bigram[u][:], mask[u][:], MULT)
 
-                entries = held.tile([P, PIECE], F32, name=f"entries{b}{i}")
-                piece_offsets = offsets[:, i * PIECE // PER_COLUMN : (i + 1) * PIECE // PER_COLUMN]
-                nc.vector.tensor_tensor(entries[:], window[b][:].indirect(piece_offsets), masked[:], ADD)
+        def look_up(u):
+            b, i = u
+            piece_offsets = offsets[:, i * PIECE // PER_COLUMN : (i + 1) * PIECE // PER_COLUMN]
+            nc.vector.tensor_tensor(entries[u][:], window[b][:].indirect(piece_offsets), masked[u][:], ADD)
 
-                nc.vector.tensor_reduce(
-                    sums[:, i * PIECE // L : (i + 1) * PIECE // L],
-                    entries[:].rearrange("c (p l) -> c p l", l=L),
-                    mybir.AxisListType.X,
-                    ADD,
-                )
-            nc.sync.dma_start(out[b * P : (b + 1) * P, :], sums[:])
+        def patch_sums(u):
+            b, i = u
+            nc.vector.tensor_reduce(
+                sums[b][:, i * PIECE // L : (i + 1) * PIECE // L],
+                entries[u][:].rearrange("c (p l) -> c p l", l=L),
+                mybir.AxisListType.X,
+                ADD,
+            )
+
+        product(units[0])
+        for k, u in enumerate(units):
+            look_up(u)
+            if k + 1 < len(units):
+                product(units[k + 1])
+            patch_sums(u)
+            b, i = u
+            if i == PIECES - 1:
+                nc.sync.dma_start(out[b * P : (b + 1) * P, :], sums[b][:])

@@ -40,7 +40,7 @@ def tile_patchembedder_kernel(tc, table, h, hmask, offs, out):
                 (nc.sync, nc.scalar)[b % 2].dma_start(window[b][:], table[rows, :])
 
         def product(u):
-            nc.vector.tensor_tensor(masked[u][:], bigram[u][:], mask[u][:], MULT)
+            nc.gpsimd.tensor_tensor(masked[u][:], bigram[u][:], mask[u][:], MULT)
 
         def look_up(u):
             b, i = u
@@ -56,11 +56,9 @@ def tile_patchembedder_kernel(tc, table, h, hmask, offs, out):
                 ADD,
             )
 
-        product(units[0])
-        for k, u in enumerate(units):
+        for u in units:
+            product(u)
             look_up(u)
-            if k + 1 < len(units):
-                product(units[k + 1])
             patch_sums(u)
             b, i = u
             if i == PIECES - 1:

@@ -24,7 +24,7 @@ def tile_patchembedder_kernel(tc, table, h, hmask, offs, out):
         offsets = held.tile([P, N // PER_COLUMN], U16, name="offsets")
         window = [held.tile([P, S], F32, name=f"window{b}") for b in range(BLOCKS)]
         sums = [held.tile([P, N // L], F32, name=f"sums{b}") for b in range(BLOCKS)]
-        mask = {u: held.tile([P, PIECE], F32, name=f"mask{u[0]}{u[1]}") for u in units}
+        mask = [held.tile([P, PIECE], F32, name=f"mask{i}") for i in range(PIECES)]
         bigram = {u: held.tile([P, PIECE], F32, name=f"bigram{u[0]}{u[1]}") for u in units}
         masked = {u: held.tile([P, PIECE], F32, name=f"masked{u[0]}{u[1]}") for u in units}
         entries = {u: held.tile([P, PIECE], F32, name=f"entries{u[0]}{u[1]}") for u in units}
@@ -32,15 +32,16 @@ def tile_patchembedder_kernel(tc, table, h, hmask, offs, out):
         for b, i in units:
             rows = slice(b * P, (b + 1) * P)
             cols = slice(i * PIECE, (i + 1) * PIECE)
-            nc.sync.dma_start(mask[b, i][:], hmask[rows, cols])
+            if b == 0:
+                nc.sync.dma_start(mask[i][:], hmask[rows, cols])
             nc.scalar.dma_start(bigram[b, i][:], h[rows, cols])
             if i == 0:
                 if b == 0:
                     nc.sync.dma_start(offsets[:], offs)
-                (nc.sync, nc.scalar)[b % 2].dma_start(window[b][:], table[rows, :])
+                nc.sync.dma_start(window[b][:], table[rows, :])
 
         def product(u):
-            nc.gpsimd.tensor_tensor(masked[u][:], bigram[u][:], mask[u][:], MULT)
+            nc.vector.tensor_tensor(masked[u][:], bigram[u][:], mask[u[1]][:], MULT)
 
         def look_up(u):
             b, i = u
@@ -56,9 +57,11 @@ def tile_patchembedder_kernel(tc, table, h, hmask, offs, out):
                 ADD,
             )
 
-        for u in units:
-            product(u)
+        product(units[0])
+        for k, u in enumerate(units):
             look_up(u)
+            if k + 1 < len(units):
+                product(units[k + 1])
             patch_sums(u)
             b, i = u
             if i == PIECES - 1:

@@ -13,56 +13,47 @@ L = 8
 PIECE = S
 PER_COLUMN = 16
 BLOCKS = C // P
-PIECES = N // PIECE
 
 
 def tile_patchembedder_kernel(tc, table, h, hmask, offs, out):
     nc = tc.nc
-    units = [(b, i) for b in range(BLOCKS) for i in range(PIECES)]
-
     with tc.tile_pool(name="held", bufs=1) as held:
         offsets = held.tile([P, N // PER_COLUMN], U16, name="offsets")
         window = [held.tile([P, S], F32, name=f"window{b}") for b in range(BLOCKS)]
+        mask = [held.tile([P, N], F32, name=f"mask{b}") for b in range(BLOCKS)]
+        bigram = [held.tile([P, N], F32, name=f"bigram{b}") for b in range(BLOCKS)]
+        masked = [held.tile([P, N], F32, name=f"masked{b}") for b in range(BLOCKS)]
+        entries = [held.tile([P, N], F32, name=f"entries{b}") for b in range(BLOCKS)]
         sums = [held.tile([P, N // L], F32, name=f"sums{b}") for b in range(BLOCKS)]
-        mask = [held.tile([P, PIECE], F32, name=f"mask{i}") for i in range(PIECES)]
-        bigram = {u: held.tile([P, PIECE], F32, name=f"bigram{u[0]}{u[1]}") for u in units}
-        masked = {u: held.tile([P, PIECE], F32, name=f"masked{u[0]}{u[1]}") for u in units}
-        entries = {u: held.tile([P, PIECE], F32, name=f"entries{u[0]}{u[1]}") for u in units}
 
-        for b, i in units:
+        for b in range(BLOCKS):
             rows = slice(b * P, (b + 1) * P)
-            cols = slice(i * PIECE, (i + 1) * PIECE)
+            nc.sync.dma_start(mask[b][:], hmask[rows, :])
+            nc.scalar.dma_start(bigram[b][:], h[rows, :])
             if b == 0:
-                nc.sync.dma_start(mask[i][:], hmask[rows, cols])
-            nc.scalar.dma_start(bigram[b, i][:], h[rows, cols])
-            if i == 0:
-                if b == 0:
-                    nc.sync.dma_start(offsets[:], offs)
-                nc.sync.dma_start(window[b][:], table[rows, :])
+                nc.sync.dma_start(offsets[:], offs)
+            (nc.scalar, nc.sync)[b % 2].dma_start(window[b][:], table[rows, :])
 
-        def product(u):
-            nc.vector.tensor_tensor(masked[u][:], bigram[u][:], mask[u[1]][:], MULT)
+        def product(b):
+            nc.vector.tensor_tensor(masked[b][:], bigram[b][:], mask[b][:], MULT)
 
-        def look_up(u):
-            b, i = u
-            piece_offsets = offsets[:, i * PIECE // PER_COLUMN : (i + 1) * PIECE // PER_COLUMN]
-            nc.vector.tensor_tensor(entries[u][:], window[b][:].indirect(piece_offsets), masked[u][:], ADD)
-
-        def patch_sums(u):
-            b, i = u
-            nc.vector.tensor_reduce(
-                sums[b][:, i * PIECE // L : (i + 1) * PIECE // L],
-                entries[u][:].rearrange("c (p l) -> c p l", l=L),
-                mybir.AxisListType.X,
-                ADD,
+        def look_up(b, start):
+            piece = slice(start, start + PIECE)
+            piece_offsets = offsets[:, start // PER_COLUMN : (start + PIECE) // PER_COLUMN]
+            nc.vector.tensor_tensor(
+                entries[b][:, piece], window[b][:].indirect(piece_offsets), masked[b][:, piece], ADD
             )
 
-        product(units[0])
-        for k, u in enumerate(units):
-            look_up(u)
-            if k + 1 < len(units):
-                product(units[k + 1])
-            patch_sums(u)
-            b, i = u
-            if i == PIECES - 1:
-                nc.sync.dma_start(out[b * P : (b + 1) * P, :], sums[b][:])
+        def patch_sums(b):
+            nc.vector.tensor_reduce(
+                sums[b][:], entries[b][:].rearrange("c (p l) -> c p l", l=L), mybir.AxisListType.X, ADD
+            )
+
+        product(0)
+        for b in range(BLOCKS):
+            for start in range(0, N, PIECE):
+                look_up(b, start)
+            if b + 1 < BLOCKS:
+                product(b + 1)
+            patch_sums(b)
+            nc.sync.dma_start(out[b * P : (b + 1) * P, :], sums[b][:])

@@ -19,23 +19,22 @@ def tile_patchembedder_kernel(tc, table, h, hmask, offs, out):
     nc = tc.nc
     with tc.tile_pool(name="held", bufs=1) as held:
         offsets = held.tile([P, N // PER_COLUMN], U16, name="offsets")
+        mask = held.tile([P, N], F32, name="mask")
         window = [held.tile([P, S], F32, name=f"window{b}") for b in range(BLOCKS)]
-        mask = [held.tile([P, N], F32, name=f"mask{b}") for b in range(BLOCKS)]
         bigram = [held.tile([P, N], F32, name=f"bigram{b}") for b in range(BLOCKS)]
         masked = [held.tile([P, N], F32, name=f"masked{b}") for b in range(BLOCKS)]
         entries = [held.tile([P, N], F32, name=f"entries{b}") for b in range(BLOCKS)]
         sums = [held.tile([P, N // L], F32, name=f"sums{b}") for b in range(BLOCKS)]
 
+        nc.sync.dma_start(mask[:], hmask[0:P, :])
+        nc.sync.dma_start(offsets[:], offs)
         for b in range(BLOCKS):
             rows = slice(b * P, (b + 1) * P)
-            nc.sync.dma_start(mask[b][:], hmask[rows, :])
             nc.scalar.dma_start(bigram[b][:], h[rows, :])
-            if b == 0:
-                nc.sync.dma_start(offsets[:], offs)
-            (nc.scalar, nc.sync)[b % 2].dma_start(window[b][:], table[rows, :])
+            nc.sync.dma_start(window[b][:], table[rows, :])
 
         def product(b):
-            nc.vector.tensor_tensor(masked[b][:], bigram[b][:], mask[b][:], MULT)
+            nc.vector.tensor_tensor(masked[b][:], bigram[b][:], mask[:], MULT)
 
         def look_up(b, start):
             piece = slice(start, start + PIECE)

@@ -48,11 +48,11 @@ def tile_patchembedder_kernel(tc, table, h, hmask, offs, out):
                 sums[b][:], entries[b][:].rearrange("c (p l) -> c p l", l=L), mybir.AxisListType.X, ADD
             )
 
-        product(0)
+        for b in range(BLOCKS):
+            product(b)
         for b in range(BLOCKS):
             for start in range(0, N, PIECE):
                 look_up(b, start)
-            if b + 1 < BLOCKS:
-                product(b + 1)
+        for b in range(BLOCKS):
             patch_sums(b)
             nc.sync.dma_start(out[b * P : (b + 1) * P, :], sums[b][:])

@@ -27,11 +27,11 @@ def tile_patchembedder_kernel(tc, table, h, hmask, offs, out):
         sums = [held.tile([P, N // L], F32, name=f"sums{b}") for b in range(BLOCKS)]
 
         nc.sync.dma_start(mask[:], hmask[0:P, :])
+        for b in range(BLOCKS):
+            nc.sync.dma_start(bigram[b][:], h[b * P : (b + 1) * P, :])
         nc.sync.dma_start(offsets[:], offs)
         for b in range(BLOCKS):
-            rows = slice(b * P, (b + 1) * P)
-            nc.scalar.dma_start(bigram[b][:], h[rows, :])
-            nc.sync.dma_start(window[b][:], table[rows, :])
+            nc.sync.dma_start(window[b][:], table[b * P : (b + 1) * P, :])
 
         def product(b):
             nc.vector.tensor_tensor(masked[b][:], bigram[b][:], mask[:], MULT)

@@ -43,16 +43,22 @@ def tile_patchembedder_kernel(tc, table, h, hmask, offs, out):
                 entries[b][:, piece], window[b][:].indirect(piece_offsets), masked[b][:, piece], ADD
             )
 
-        def patch_sums(b):
+        def patch_sums(b, start, stop):
             nc.vector.tensor_reduce(
-                sums[b][:], entries[b][:].rearrange("c (p l) -> c p l", l=L), mybir.AxisListType.X, ADD
+                sums[b][:, start // L : stop // L],
+                entries[b][:, start:stop].rearrange("c (p l) -> c p l", l=L),
+                mybir.AxisListType.X,
+                ADD,
             )
 
         for b in range(BLOCKS):
             product(b)
-        for b in range(BLOCKS):
-            for start in range(0, N, PIECE):
-                look_up(b, start)
-        for b in range(BLOCKS):
-            patch_sums(b)
-            nc.sync.dma_start(out[b * P : (b + 1) * P, :], sums[b][:])
+        look_up(0, 0)
+        look_up(0, PIECE)
+        look_up(1, 0)
+        patch_sums(0, 0, N)
+        nc.sync.dma_start(out[0:P, :], sums[0][:])
+        look_up(1, PIECE)
+        patch_sums(1, 0, PIECE)
+        patch_sums(1, PIECE, N)
+        nc.sync.dma_start(out[P:C, :], sums[1][:])

@@ -1,6 +1,7 @@
 import concourse.mybir as mybir
 
 F32 = mybir.dt.float32
+BF16 = mybir.dt.bfloat16
 U16 = mybir.dt.uint16
 ADD = mybir.AluOpType.add
 MULT = mybir.AluOpType.mult
@@ -13,32 +14,48 @@ L = 8
 PIECE = S
 PER_COLUMN = 16
 BLOCKS = C // P
+ROWS = 32
+BANK = 512
 
 
 def tile_patchembedder_kernel(tc, table, h, hmask, offs, out):
     nc = tc.nc
-    with tc.tile_pool(name="held", bufs=1) as held:
+    with tc.tile_pool(name="held", bufs=1) as held, tc.psum_pool(name="psum", bufs=1) as psum:
         offsets = held.tile([P, N // PER_COLUMN], U16, name="offsets")
-        mask = held.tile([P, N], F32, name="mask")
+        mask_rows = held.tile([ROWS, N], F32, name="mask_rows")
+        mean = held.tile([ROWS, P], BF16, name="mean")
         window = [held.tile([P, S], F32, name=f"window{b}") for b in range(BLOCKS)]
         bigram = [held.tile([P, N], F32, name=f"bigram{b}") for b in range(BLOCKS)]
         masked = [held.tile([P, N], F32, name=f"masked{b}") for b in range(BLOCKS)]
         entries = [held.tile([P, N], F32, name=f"entries{b}") for b in range(BLOCKS)]
         sums = [held.tile([P, N // L], F32, name=f"sums{b}") for b in range(BLOCKS)]
+        mask = [psum.tile([P, BANK], F32, name=f"mask{k}") for k in range(N // PIECE)]
 
-        nc.sync.dma_start(mask[:], hmask[0:P, :])
+        nc.sync.dma_start(mask_rows[:], hmask[0:ROWS, :])
         for b in range(BLOCKS):
             nc.sync.dma_start(bigram[b][:], h[b * P : (b + 1) * P, :])
         nc.sync.dma_start(offsets[:], offs)
         for b in range(BLOCKS):
             nc.sync.dma_start(window[b][:], table[b * P : (b + 1) * P, :])
 
-        def product(b):
-            nc.vector.tensor_tensor(masked[b][:], bigram[b][:], mask[:], MULT)
+        nc.vector.memset(mean[:], 1.0 / ROWS)
+        upper_halves = mask_rows[:].bitcast(BF16)[:, 1 : 2 * N : 2]
+        for k in range(N // PIECE):
+            nc.tensor.matmul(
+                mask[k][:, 0:PIECE],
+                mean[:],
+                upper_halves[:, k * PIECE : (k + 1) * PIECE],
+                start=True,
+                stop=True,
+            )
 
-        def look_up(b, start):
-            piece = slice(start, start + PIECE)
-            piece_offsets = offsets[:, start // PER_COLUMN : (start + PIECE) // PER_COLUMN]
+        def product(b, k):
+            piece = slice(k * PIECE, (k + 1) * PIECE)
+            nc.vector.tensor_tensor(masked[b][:, piece], bigram[b][:, piece], mask[k][:, 0:PIECE], MULT)
+
+        def look_up(b, k):
+            piece = slice(k * PIECE, (k + 1) * PIECE)
+            piece_offsets = offsets[:, k * PIECE // PER_COLUMN : (k + 1) * PIECE // PER_COLUMN]
             nc.vector.tensor_tensor(
                 entries[b][:, piece], window[b][:].indirect(piece_offsets), masked[b][:, piece], ADD
             )
@@ -52,13 +69,14 @@ def tile_patchembedder_kernel(tc, table, h, hmask, offs, out):
             )
 
         for b in range(BLOCKS):
-            product(b)
+            for k in range(N // PIECE):
+                product(b, k)
         look_up(0, 0)
-        look_up(0, PIECE)
+        look_up(0, 1)
         look_up(1, 0)
         patch_sums(0, 0, N)
         nc.sync.dma_start(out[0:P, :], sums[0][:])
-        look_up(1, PIECE)
+        look_up(1, 1)
         patch_sums(1, 0, PIECE)
         patch_sums(1, PIECE, N)
         nc.sync.dma_start(out[P:C, :], sums[1][:])

import concourse.mybir as mybir

F32 = mybir.dt.float32
BF16 = mybir.dt.bfloat16
U16 = mybir.dt.uint16
ADD = mybir.AluOpType.add
MULT = mybir.AluOpType.mult

P = 128
C = 256
S = 256
N = 512
L = 8
PIECE = S
PER_COLUMN = 16
BLOCKS = C // P
ROWS = 32
BANK = 512


def tile_patchembedder_kernel(tc, table, h, hmask, offs, out):
    nc = tc.nc
    with tc.tile_pool(name="held", bufs=1) as held, tc.psum_pool(name="psum", bufs=1) as psum:
        offsets = held.tile([P, N // PER_COLUMN], U16, name="offsets")
        mask_rows = held.tile([ROWS, N], F32, name="mask_rows")
        mean = held.tile([ROWS, P], BF16, name="mean")
        window = [held.tile([P, S], F32, name=f"window{b}") for b in range(BLOCKS)]
        bigram = [held.tile([P, N], F32, name=f"bigram{b}") for b in range(BLOCKS)]
        masked = [held.tile([P, N], F32, name=f"masked{b}") for b in range(BLOCKS)]
        entries = [held.tile([P, N], F32, name=f"entries{b}") for b in range(BLOCKS)]
        sums = [held.tile([P, N // L], F32, name=f"sums{b}") for b in range(BLOCKS)]
        mask = [psum.tile([P, BANK], F32, name=f"mask{k}") for k in range(N // PIECE)]

        nc.sync.dma_start(mask_rows[:], hmask[0:ROWS, :])
        for b in range(BLOCKS):
            nc.sync.dma_start(bigram[b][:], h[b * P : (b + 1) * P, :])
        nc.sync.dma_start(offsets[:], offs)
        for b in range(BLOCKS):
            nc.sync.dma_start(window[b][:], table[b * P : (b + 1) * P, :])

        nc.vector.memset(mean[:], 1.0 / ROWS)
        upper_halves = mask_rows[:].bitcast(BF16)[:, 1 : 2 * N : 2]
        for k in range(N // PIECE):
            nc.tensor.matmul(
                mask[k][:, 0:PIECE],
                mean[:],
                upper_halves[:, k * PIECE : (k + 1) * PIECE],
                start=True,
                stop=True,
            )

        def product(b, k):
            piece = slice(k * PIECE, (k + 1) * PIECE)
            nc.vector.tensor_tensor(masked[b][:, piece], bigram[b][:, piece], mask[k][:, 0:PIECE], MULT)

        def look_up(b, k):
            piece = slice(k * PIECE, (k + 1) * PIECE)
            piece_offsets = offsets[:, k * PIECE // PER_COLUMN : (k + 1) * PIECE // PER_COLUMN]
            nc.vector.tensor_tensor(
                entries[b][:, piece], window[b][:].indirect(piece_offsets), masked[b][:, piece], ADD
            )

        def patch_sums(b, start, stop):
            nc.vector.tensor_reduce(
                sums[b][:, start // L : stop // L],
                entries[b][:, start:stop].rearrange("c (p l) -> c p l", l=L),
                mybir.AxisListType.X,
                ADD,
            )

        for b in range(BLOCKS):
            for k in range(N // PIECE):
                product(b, k)
        look_up(0, 0)
        look_up(0, 1)
        look_up(1, 0)
        patch_sums(0, 0, N)
        nc.sync.dma_start(out[0:P, :], sums[0][:])
        look_up(1, 1)
        patch_sums(1, 0, PIECE)
        patch_sums(1, PIECE, N)
        nc.sync.dma_start(out[P:C, :], sums[1][:])
